import numpy as np
import ml_dtypes


def mxq(x, axis, fmt="e4m3"):
    dtype, down = {"e4m3": (ml_dtypes.float8_e4m3fn, 7), "e5m2": (ml_dtypes.float8_e5m2, 14)}[fmt]
    v = np.moveaxis(np.asarray(x, np.float32).astype(ml_dtypes.bfloat16).astype(np.float64), axis, -1)
    blocks = v.reshape(v.shape[:-1] + (-1, 32))
    amax = np.abs(blocks).max(-1, keepdims=True)
    byte = np.maximum(np.where(amax > 0, np.frexp(amax)[1] - 1 + 127, 0) - down, 1)
    scale = np.exp2(byte - 127.0)
    codes = (blocks / scale).astype(np.float32).astype(dtype).astype(np.float64)
    return np.moveaxis((codes * scale).reshape(v.shape), -1, axis)


WIDE = False


def mx_kscale(k):
    if not WIDE:
        return np.ones(k)
    levels = np.array([10, -10, 5, -5, 0])
    a = np.random.permutation(np.resize(levels, k // 512 * 4)).reshape(k // 512, 4)
    idx = np.arange(k)
    return np.exp2(a[idx // 512, idx % 128 // 32])


BF16 = ml_dtypes.bfloat16


def bf(x):
    return np.asarray(x, np.float32).astype(BF16)


def f64(x):
    return np.asarray(x).astype(np.float64)


B, V, H = 512, 128, 1024
G = 4 * H
EPS = 1e-5


def sigmoid(v):
    return 1.0 / (1.0 + np.exp(-v))


def layer_norm(v, w, b):
    mu = v.mean(-1, keepdims=True)
    var = ((v - mu) ** 2).mean(-1, keepdims=True)
    return (v - mu) / np.sqrt(var + EPS) * w + b


def setup_inputs():
    s = mx_kscale(H)
    return {"x": bf(np.random.standard_normal((B, V))),
            "h0": bf(np.random.standard_normal((B, H)) * s),
            "c0": bf(np.random.standard_normal((B, H))),
            "w_ih1": bf(np.random.standard_normal((G, V)) / np.sqrt(V)),
            "w_hh1": bf(np.random.standard_normal((G, H)) / np.sqrt(H) / s),
            "lni_w1": bf(1.0 + 0.1 * np.random.standard_normal(G)),
            "lni_b1": bf(0.1 * np.random.standard_normal(G)),
            "lnh_w1": bf(1.0 + 0.1 * np.random.standard_normal(G)),
            "lnh_b1": bf(0.1 * np.random.standard_normal(G)),
            "lnc_w1": bf(1.0 + 0.1 * np.random.standard_normal(H)),
            "lnc_b1": bf(0.1 * np.random.standard_normal(H))}


def reference(x, h0, c0, w_ih1, w_hh1, lni_w1, lni_b1, lnh_w1, lnh_b1, lnc_w1, lnc_b1):
    a = f64(x) @ f64(w_ih1).T
    r = mxq(f64(h0), 1, "e4m3") @ mxq(f64(w_hh1), 1, "e4m3").T
    gates = layer_norm(a, f64(lni_w1), f64(lni_b1)) + layer_norm(r, f64(lnh_w1), f64(lnh_b1))
    i, f, g, o = np.split(gates, 4, axis=1)
    cy = layer_norm(sigmoid(f) * f64(c0) + sigmoid(i) * np.tanh(g), f64(lnc_w1), f64(lnc_b1))
    hy = sigmoid(o) * np.tanh(cy)
    return hy, cy

@@ -1,0 +1,413 @@
+from contextlib import ExitStack
+
+import concourse.mybir as mybir
+from concourse.masks import make_identity
+
+F32 = mybir.dt.float32
+BF16 = mybir.dt.bfloat16
+U32 = mybir.dt.uint32
+U8 = mybir.dt.uint8
+FP8X4 = mybir.dt.float8_e4m3fn_x4
+ACT = mybir.ActivationFunctionType
+ALU = mybir.AluOpType
+
+P = 128
+B, V, H = 512, 128, 1024
+G = 4 * H
+EPS = 1e-5
+UNITS = B // P
+BANK = 512
+NB = G // BANK
+FLOPS = 2 * B * G * (H + V)
+PIN = True
+POOL_UNITS = (0, 1, 2)
+
+
+def tile_multilstm_pa_kernel(
+    tc, x, h0, c0, w_ih1, w_hh1, lni_w1, lni_b1, lnh_w1, lnh_b1, lnc_w1, lnc_b1, out_0, out_1
+):
+    nc = tc.nc
+    with ExitStack() as ctx:
+        if PIN:
+            ctx.enter_context(tc.manual_schedule())
+        const = ctx.enter_context(tc.tile_pool(name="const", bufs=1))
+        ld = ctx.enter_context(tc.tile_pool(name="ld", bufs=4))
+        grp_pool = ctx.enter_context(tc.tile_pool(name="grp", bufs=4))
+        big = ctx.enter_context(tc.tile_pool(name="big", bufs=6))
+        small = ctx.enter_context(tc.tile_pool(name="small", bufs=4))
+        ps_t = ctx.enter_context(tc.psum_pool(name="ps_t", bufs=2))
+        ps_a = ctx.enter_context(tc.psum_pool(name="ps_a", bufs=3))
+        ps_r = ctx.enter_context(tc.psum_pool(name="ps_r", bufs=3))
+
+        x_sb = const.tile([P, UNITS, V], BF16)
+        nc.sync.dma_start(out=x_sb[:], in_=x.rearrange("(u p) v -> p u v", p=P))
+        wih_sb = ld.tile([P, G // P, V], BF16, tag="ld")
+        nc.sync.dma_start(out=wih_sb[:], in_=w_ih1.rearrange("(t p) v -> p t v", p=P))
+        bi_b = ld.tile([P, G], BF16, tag="ld")
+        nc.sync.dma_start(out=bi_b[:], in_=lni_b1.partition_broadcast(P))
+        bh_b = ld.tile([P, G], BF16, tag="ld")
+        nc.sync.dma_start(out=bh_b[:], in_=lnh_b1.partition_broadcast(P))
+        wi_b = const.tile([P, G], BF16)
+        nc.sync.dma_start(out=wi_b[:], in_=lni_w1.partition_broadcast(P))
+        h0_sb = ld.tile([P, UNITS, H], BF16, tag="ld")
+        nc.sync.dma_start(out=h0_sb[:], in_=h0.rearrange("(u p) k -> p u k", p=P))
+
+        ident_b = const.tile([P, P], BF16)
+        make_identity(nc, ident_b[:])
+        ident_f = const.tile([P, P], F32)
+        make_identity(nc, ident_f[:])
+        neghalf = const.tile([P, UNITS], F32)
+        nc.vector.memset(neghalf[:], -0.5)
+
+        xT = const.tile([P, B], BF16)
+        xT_f = const.tile([P, B], F32)
+        gram = const.tile([P, V + 4], F32)
+        tpx = ps_t.tile([P, UNITS, P], BF16, tag="tp")
+        for u in range(UNITS):
+            nc.tensor.transpose(tpx[:, u, :], x_sb[:, u, :], ident_b[:])
+        nc.scalar.copy(out=xT[:], in_=tpx[:].rearrange("p u b -> p (u b)"))
+        nc.scalar.copy(out=xT_f[:], in_=tpx[:].rearrange("p u b -> p (u b)"))
+        wihT = const.tile([P, G], BF16)
+        for q in range(4):
+            tpw = ps_t.tile([P, 8, P], BF16, tag="tp")
+            for j in range(8):
+                nc.tensor.transpose(tpw[:, j, :], wih_sb[:, 8 * q + j, :], ident_b[:])
+            nc.scalar.activation(
+                out=wihT[:, q * 1024 : (q + 1) * 1024],
+                in_=tpw[:].rearrange("p j g -> p (j g)"),
+                func=ACT.Identity,
+                accum_out=gram[:, V + q : V + q + 1],
+            )
+        gram_ps = ps_r.tile([P, V], F32, tag="mmr")
+        for t in range(G // P):
+            nc.tensor.matmul(
+                out=gram_ps[:], lhsT=wih_sb[:, t, :], rhs=wih_sb[:, t, :], start=(t == 0), stop=(t == G // P - 1)
+            )
+        nc.scalar.copy(out=gram[:, 0:V], in_=gram_ps[:])
+
+        bs = const.tile([P, G], F32)
+        for k in range(2):
+            cols = slice(k * 2048, (k + 1) * 2048)
+            nc.vector.tensor_tensor(out=bs[:, cols], in0=bi_b[:, cols], in1=bh_b[:, cols], op=ALU.add)
+
+        whh_tiles = {}
+
+        def load_whh(n):
+            whh_sb = ld.tile([P, 4, H], BF16, tag="ld")
+            nc.sync.dma_start(
+                out=whh_sb[:], in_=w_hh1[n * BANK : (n + 1) * BANK, :].rearrange("(t p) k -> p t k", p=P)
+            )
+            whh_tiles[n] = whh_sb
+
+        load_whh(0)
+        load_whh(1)
+        load_whh(2)
+
+        q4 = small.tile([P, UNITS], F32, tag="q4")
+        mean4 = small.tile([P, UNITS], F32, tag="mean4")
+        for u in range(UNITS):
+            y_ps = ps_r.tile([P, V + 4], F32, tag="mmr")
+            nc.tensor.matmul(out=y_ps[:], lhsT=xT_f[:, u * P : (u + 1) * P], rhs=gram[:], start=True, stop=True)
+            yjunk = small.tile([P, V], F32, tag="yjunk")
+            nc.vector.scalar_tensor_tensor(
+                out=yjunk[:], in0=y_ps[:, 0:V], scalar=1.0 / G, in1=x_sb[:, u, :], op0=ALU.mult, op1=ALU.mult,
+                accum_out=q4[:, u : u + 1],
+            )
+            mjunk = small.tile([P, 4], F32, tag="mjunk")
+            nc.vector.tensor_scalar(
+                out=mjunk[:], in0=y_ps[:, V : V + 4], scalar1=1.0 / G, scalar2=None, op0=ALU.mult, op1=ALU.add,
+                accum_out=mean4[:, u : u + 1],
+            )
+        msq4 = small.tile([P, UNITS], F32, tag="msq4")
+        nc.vector.tensor_tensor(out=msq4[:], in0=mean4[:], in1=mean4[:], op=ALU.mult)
+        var4 = small.tile([P, UNITS], F32, tag="var4")
+        nc.vector.tensor_tensor(out=var4[:], in0=q4[:], in1=msq4[:], op=ALU.subtract)
+        veps4 = small.tile([P, UNITS], F32, tag="veps4")
+        nc.gpsimd.tensor_scalar(out=veps4[:], in0=var4[:], scalar1=0.0, scalar2=EPS, op0=ALU.max, op1=ALU.add)
+        rstd4 = small.tile([P, UNITS], F32, tag="rstd4")
+        nc.gpsimd.tensor_tensor(out=rstd4[:], in0=veps4[:], in1=neghalf[:], op=ALU.pow)
+
+        h_codes = const.tile([P, 2, B], U32, align_bytes=64)
+        h_scales = const.tile([P, 2, B], U8, align_bytes=64)
+        w_codes = const.tile([P, 2, G], U32, align_bytes=64)
+        w_scales = const.tile([P, 2, G], U8, align_bytes=64)
+        grp_tiles = {}
+
+        def transpose_rows(key, src_words):
+            for c in range(2):
+                grp = grp_pool.tile([P, 4 * BANK], BF16, tag="grp", align_bytes=64)
+                grpw = grp[:].bitcast(F32).rearrange("p (r s) -> p r s", s=2)
+                for half in range(2):
+                    tp = ps_t.tile([P, 2, 256], F32, tag="tp")
+                    for s in range(2):
+                        for j in range(2):
+                            lo = 256 * c + 128 * s
+                            nc.tensor.transpose(
+                                tp[:, s, j * P : (j + 1) * P], src_words[:, 2 * half + j, lo : lo + P], ident_f[:]
+                            )
+                    nc.scalar.copy(
+                        out=grpw[:, half * 256 : (half + 1) * 256, :], in_=tp[:].rearrange("p s r -> p r s")
+                    )
+                grp_tiles[(key, c)] = grp
+
+        def quantise(key, codes, scales):
+            for c in range(2):
+                nc.vector.quantize_mx(
+                    out=codes[:, c, :].bitcast(FP8X4), scales=scales[:, c, :], in_=grp_tiles[(key, c)][:]
+                )
+
+        def prep_whh(n):
+            transpose_rows(n, whh_tiles[n][:].bitcast(F32))
+            if n + 4 < NB:
+                load_whh(n + 4)
+
+        def quantise_whh(n):
+            cols = slice(n * BANK, (n + 1) * BANK)
+            quantise(n, w_codes[:, :, cols], w_scales[:, :, cols])
+
+        a_tiles = {}
+        a_banks = {}
+
+        def a_matmul(k):
+            if k >= UNITS * NB:
+                return
+            u, n = divmod(k, NB)
+            acc = ps_a.tile([P, BANK], F32, tag="mma")
+            nc.tensor.matmul(
+                out=acc[:], lhsT=xT[:, u * P : (u + 1) * P], rhs=wihT[:, n * BANK : (n + 1) * BANK],
+                start=True, stop=True,
+            )
+            a_banks[k] = acc
+
+        def t1(k):
+            u, n = divmod(k, NB)
+            if n == 0:
+                a_new = big.tile([P, G], F32, tag="big")
+                a_tiles[u] = a_new
+            cols = slice(n * BANK, (n + 1) * BANK)
+            nc.vector.scalar_tensor_tensor(
+                out=a_tiles[u][:, cols], in0=a_banks[k][:], scalar=mean4[:, u : u + 1], in1=wi_b[:, cols],
+                op0=ALU.subtract, op1=ALU.mult,
+            )
+
+        def t1_group(g):
+            for k in range(4 * g, 4 * g + 4):
+                t1(k)
+                a_matmul(k + 3)
+
+        def c1(g):
+            u, half = divmod(g, 2)
+            cols = slice(half * 2048, (half + 1) * 2048)
+            nc.vector.scalar_tensor_tensor(
+                out=a_tiles[u][:, cols], in0=a_tiles[u][:, cols], scalar=rstd4[:, u : u + 1], in1=bs[:, cols],
+                op0=ALU.mult, op1=ALU.add,
+            )
+
+        r_tiles = {}
+        st = {}
+
+        def r_evict(u, banks):
+            rows = slice(u * P, (u + 1) * P)
+            if u not in r_tiles:
+                r_new = big.tile([P, G], F32, tag="big")
+                r_tiles[u] = r_new
+                s1 = small.tile([P, NB], F32, tag="s1")
+                st[("s1", u)] = s1
+            for n in banks:
+                cols = slice(n * BANK, (n + 1) * BANK)
+                acc = ps_r.tile([P, BANK], F32, tag="mmr")
+                for c in range(2):
+                    nc.tensor.matmul_mx(
+                        out=acc[:],
+                        lhsT=h_codes[:, c, rows].bitcast(FP8X4),
+                        lhsT_scale=h_scales[:, c, rows],
+                        rhs=w_codes[:, c, cols].bitcast(FP8X4),
+                        rhs_scale=w_scales[:, c, cols],
+                        start=(c == 0),
+                        stop=(c == 1),
+                    )
+                nc.scalar.activation(
+                    out=r_tiles[u][:, cols], in_=acc[:], func=ACT.Identity, accum_out=st[("s1", u)][:, n : n + 1]
+                )
+
+        def r_mean(u):
+            s1junk = small.tile([P, NB], F32, tag="s1junk")
+            negmean = small.tile([P, 1], F32, tag="negmean")
+            nc.scalar.activation(
+                out=s1junk[:], in_=st[("s1", u)][:], func=ACT.Identity, scale=-1.0 / G, accum_out=negmean[:]
+            )
+            s1junk2 = small.tile([P, NB], F32, tag="s1junk2")
+            negmean64 = small.tile([P, 1], F32, tag="negmean64")
+            nc.scalar.activation(
+                out=s1junk2[:], in_=st[("s1", u)][:], func=ACT.Identity, scale=-1.0 / (G * 64.0), accum_out=negmean64[:]
+            )
+            ssq = small.tile([P, 2], F32, tag="ssq")
+            st[("negmean", u)] = negmean
+            st[("negmean64", u)] = negmean64
+            st[("ssq", u)] = ssq
+
+        def r_var(u, k):
+            junk = grp_pool.tile([P, 2048], BF16, tag="grp", align_bytes=64)
+            nc.scalar.activation(
+                out=junk[:], in_=r_tiles[u][:, k * 2048 : (k + 1) * 2048], func=ACT.Square,
+                bias=st[("negmean64", u)][:, 0:1], scale=1.0 / 64.0, accum_out=st[("ssq", u)][:, k : k + 1],
+            )
+            if k == 1:
+                ssq = st[("ssq", u)]
+                veps = small.tile([P, 1], F32, tag="veps")
+                nc.gpsimd.tensor_scalar(
+                    out=veps[:], in0=ssq[:, 0:1], scalar1=ssq[:, 1:2], scalar2=EPS, op0=ALU.add, op1=ALU.add
+                )
+                rstd = small.tile([P, 1], F32, tag="rstd")
+                nc.gpsimd.tensor_tensor(out=rstd[:], in0=veps[:], in1=neghalf[:, 0:1], op=ALU.pow)
+                st[("rstd", u)] = rstd
+
+        def t2(u, k):
+            cols = slice(k * H, (k + 1) * H)
+            nc.vector.scalar_tensor_tensor(
+                out=r_tiles[u][:, cols], in0=r_tiles[u][:, cols], scalar=st[("negmean", u)][:, 0:1],
+                in1=wh_b[:, cols], op0=ALU.add, op1=ALU.mult,
+            )
+
+        funcs = [ACT.Sigmoid, ACT.Sigmoid, ACT.Tanh, ACT.Sigmoid]
+
+        def c2(u, k):
+            cols = slice(k * H, (k + 1) * H)
+            nc.vector.scalar_tensor_tensor(
+                out=r_tiles[u][:, cols], in0=r_tiles[u][:, cols], scalar=st[("rstd", u)][:, 0:1],
+                in1=a_tiles[u][:, cols], op0=ALU.mult, op1=ALU.add,
+            )
+            nc.scalar.activation(out=r_tiles[u][:, cols], in_=r_tiles[u][:, cols], func=funcs[k])
+
+        def gate(u, k):
+            return r_tiles[u][:, k * H : (k + 1) * H]
+
+        def side(u):
+            return nc.gpsimd if u in POOL_UNITS else nc.vector
+
+        def m1(u):
+            side(u).tensor_tensor(out=gate(u, 1), in0=gate(u, 1), in1=c0_sb[:, u, :], op=ALU.mult)
+
+        def m2_cp(u):
+            nc.vector.tensor_tensor(out=gate(u, 0), in0=gate(u, 0), in1=gate(u, 2), op=ALU.mult)
+            csum = small.tile([P, 1], F32, tag="csum")
+            nc.vector.scalar_tensor_tensor(
+                out=gate(u, 0), in0=gate(u, 0), scalar=1.0, in1=gate(u, 1), op0=ALU.mult, op1=ALU.add,
+                accum_out=csum[:],
+            )
+            cneg = small.tile([P, 2], F32, tag="cneg")
+            nc.vector.tensor_scalar(out=cneg[:, 0:1], in0=csum[:], scalar1=-1.0 / H, scalar2=None, op0=ALU.mult)
+            nc.vector.tensor_scalar(
+                out=cneg[:, 1:2], in0=csum[:], scalar1=-1.0 / (H * 32.0), scalar2=None, op0=ALU.mult
+            )
+            st[("cneg", u)] = cneg
+
+        def c_var(u):
+            cssq = small.tile([P, 1], F32, tag="cssq")
+            cjunk = grp_pool.tile([P, 2048], BF16, tag="grp", align_bytes=64)
+            nc.scalar.activation(
+                out=cjunk[:, 0:H], in_=gate(u, 0), func=ACT.Square, bias=st[("cneg", u)][:, 1:2], scale=1.0 / 32.0,
+                accum_out=cssq[:],
+            )
+            cveps = small.tile([P, 1], F32, tag="cveps")
+            nc.gpsimd.tensor_scalar(out=cveps[:], in0=cssq[:], scalar1=EPS, scalar2=0.0, op0=ALU.add, op1=ALU.add)
+            crstd = small.tile([P, 1], F32, tag="crstd")
+            nc.gpsimd.tensor_tensor(out=crstd[:], in0=cveps[:], in1=neghalf[:, 0:1], op=ALU.pow)
+            st[("crstd", u)] = crstd
+
+        def cy1(u):
+            nc.vector.scalar_tensor_tensor(
+                out=gate(u, 2), in0=gate(u, 0), scalar=st[("cneg", u)][:, 0:1], in1=lwlb[:, 0, :],
+                op0=ALU.add, op1=ALU.mult,
+            )
+
+        def cy(u):
+            nc.vector.scalar_tensor_tensor(
+                out=gate(u, 1), in0=gate(u, 2), scalar=st[("crstd", u)][:, 0:1], in1=lwlb[:, 1, :],
+                op0=ALU.mult, op1=ALU.add,
+            )
+            nc.sync.dma_start(out=out_1[u * P : (u + 1) * P, :], in_=gate(u, 1))
+
+        def c_tanh(u):
+            nc.scalar.activation(out=gate(u, 0), in_=gate(u, 1), func=ACT.Tanh)
+
+        def hy(u):
+            side(u).tensor_tensor(out=gate(u, 3), in0=gate(u, 3), in1=gate(u, 0), op=ALU.mult)
+            nc.sync.dma_start(out=out_0[u * P : (u + 1) * P, :], in_=gate(u, 3))
+
+        for k in range(3):
+            a_matmul(k)
+        transpose_rows("h", h0_sb[:].bitcast(F32))
+        load_whh(3)
+        prep_whh(0)
+        t1_group(0)
+        c1(0)
+        quantise("h", h_codes, h_scales)
+        prep_whh(1)
+        quantise_whh(0)
+        prep_whh(2)
+        for g in range(1, 4):
+            t1_group(g)
+            quantise_whh(2 * g - 1)
+            prep_whh(2 * g + 1)
+            c1(g)
+            quantise_whh(2 * g)
+            if 2 * g + 2 < NB:
+                prep_whh(2 * g + 2)
+        wh_b = ld.tile([P, G], BF16, tag="ld")
+        nc.sync.dma_start(out=wh_b[:], in_=lnh_w1.partition_broadcast(P))
+        lwlb = ld.tile([P, 2, H], BF16, tag="ld")
+        nc.sync.dma_start(out=lwlb[:, 0, :], in_=lnc_w1.partition_broadcast(P))
+        nc.sync.dma_start(out=lwlb[:, 1, :], in_=lnc_b1.partition_broadcast(P))
+        c0_sb = ld.tile([P, UNITS, H], BF16, tag="ld")
+        nc.sync.dma_start(out=c0_sb[:], in_=c0.rearrange("(u p) k -> p u k", p=P))
+        t1_group(4)
+        quantise_whh(7)
+        r_evict(0, range(NB))
+        r_mean(0)
+        c1(4)
+        t1_group(5)
+        r_var(0, 0)
+        r_var(0, 1)
+        c1(5)
+        r_evict(1, range(NB))
+        r_mean(1)
+        t1_group(6)
+        c1(6)
+        r_var(1, 0)
+        r_var(1, 1)
+        t1_group(7)
+        c1(7)
+
+        for k in range(4):
+            t2(0, k)
+        for u in range(UNITS):
+            nxt = u + 1 < UNITS
+            far = u + 2 < UNITS
+            c2(u, 1)
+            m1(u)
+            c2(u, 0)
+            c2(u, 2)
+            c2(u, 3)
+            if far:
+                r_evict(u + 2, range(0, 6))
+            if nxt:
+                t2(u + 1, 0)
+                t2(u + 1, 1)
+            m2_cp(u)
+            c_var(u)
+            if far:
+                r_evict(u + 2, range(6, NB))
+                r_mean(u + 2)
+            if nxt:
+                t2(u + 1, 2)
+            cy1(u)
+            if nxt:
+                t2(u + 1, 3)
+            if far:
+                r_var(u + 2, 0)
+            cy(u)
+            c_tanh(u)
+            if far:
+                r_var(u + 2, 1)
+            hy(u)

@@ -20,7 +20,7 @@ BANK = 512
 NB = G // BANK
 FLOPS = 2 * B * G * (H + V)
 PIN = True
-POOL_UNITS = (0, 1, 2)
+POOL_UNITS = ()
 
 
 def tile_multilstm_pa_kernel(
@@ -43,12 +43,12 @@ def tile_multilstm_pa_kernel(
         nc.sync.dma_start(out=x_sb[:], in_=x.rearrange("(u p) v -> p u v", p=P))
         wih_sb = ld.tile([P, G // P, V], BF16, tag="ld")
         nc.sync.dma_start(out=wih_sb[:], in_=w_ih1.rearrange("(t p) v -> p t v", p=P))
-        bi_b = ld.tile([P, G], BF16, tag="ld")
-        nc.sync.dma_start(out=bi_b[:], in_=lni_b1.partition_broadcast(P))
-        bh_b = ld.tile([P, G], BF16, tag="ld")
-        nc.sync.dma_start(out=bh_b[:], in_=lnh_b1.partition_broadcast(P))
         wi_b = const.tile([P, G], BF16)
-        nc.sync.dma_start(out=wi_b[:], in_=lni_w1.partition_broadcast(P))
+        nc.scalar.dma_start(out=wi_b[:], in_=lni_w1.partition_broadcast(P))
+        bi_b = ld.tile([P, G], BF16, tag="ld")
+        nc.scalar.dma_start(out=bi_b[:], in_=lni_b1.partition_broadcast(P))
+        bh_b = ld.tile([P, G], BF16, tag="ld")
+        nc.scalar.dma_start(out=bh_b[:], in_=lnh_b1.partition_broadcast(P))
         h0_sb = ld.tile([P, UNITS, H], BF16, tag="ld")
         nc.sync.dma_start(out=h0_sb[:], in_=h0.rearrange("(u p) k -> p u k", p=P))
 
@@ -254,10 +254,9 @@ def tile_multilstm_pa_kernel(
             )
             if k == 1:
                 ssq = st[("ssq", u)]
+                vjunk = small.tile([P, 2], F32, tag="vjunk")
                 veps = small.tile([P, 1], F32, tag="veps")
-                nc.gpsimd.tensor_scalar(
-                    out=veps[:], in0=ssq[:, 0:1], scalar1=ssq[:, 1:2], scalar2=EPS, op0=ALU.add, op1=ALU.add
-                )
+                nc.scalar.activation(out=vjunk[:], in_=ssq[:], func=ACT.Identity, bias=EPS / 2.0, accum_out=veps[:])
                 rstd = small.tile([P, 1], F32, tag="rstd")
                 nc.gpsimd.tensor_tensor(out=rstd[:], in0=veps[:], in1=neghalf[:, 0:1], op=ALU.pow)
                 st[("rstd", u)] = rstd
@@ -310,7 +309,7 @@ def tile_multilstm_pa_kernel(
                 accum_out=cssq[:],
             )
             cveps = small.tile([P, 1], F32, tag="cveps")
-            nc.gpsimd.tensor_scalar(out=cveps[:], in0=cssq[:], scalar1=EPS, scalar2=0.0, op0=ALU.add, op1=ALU.add)
+            nc.scalar.activation(out=cveps[:], in_=cssq[:], func=ACT.Identity, bias=EPS)
             crstd = small.tile([P, 1], F32, tag="crstd")
             nc.gpsimd.tensor_tensor(out=crstd[:], in0=cveps[:], in1=neghalf[:, 0:1], op=ALU.pow)
             st[("crstd", u)] = crstd
@@ -385,21 +384,23 @@ def tile_multilstm_pa_kernel(
             nxt = u + 1 < UNITS
             far = u + 2 < UNITS
             c2(u, 1)
-            m1(u)
             c2(u, 0)
             c2(u, 2)
             c2(u, 3)
+            if u > 0:
+                hy(u - 1)
             if far:
                 r_evict(u + 2, range(0, 6))
             if nxt:
                 t2(u + 1, 0)
-                t2(u + 1, 1)
+            m1(u)
             m2_cp(u)
             c_var(u)
             if far:
                 r_evict(u + 2, range(6, NB))
                 r_mean(u + 2)
             if nxt:
+                t2(u + 1, 1)
                 t2(u + 1, 2)
             cy1(u)
             if nxt:
@@ -410,4 +411,4 @@ def tile_multilstm_pa_kernel(
             c_tanh(u)
             if far:
                 r_var(u + 2, 1)
-            hy(u)
+        hy(UNITS - 1)

@@ -20,6 +20,7 @@ BANK = 512
 NB = G // BANK
 FLOPS = 2 * B * G * (H + V)
 PIN = True
+A_BANKS = 4
 POOL_UNITS = ()
 
 
@@ -36,21 +37,35 @@ def tile_multilstm_pa_kernel(
         big = ctx.enter_context(tc.tile_pool(name="big", bufs=6))
         small = ctx.enter_context(tc.tile_pool(name="small", bufs=4))
         ps_t = ctx.enter_context(tc.psum_pool(name="ps_t", bufs=2))
-        ps_a = ctx.enter_context(tc.psum_pool(name="ps_a", bufs=3))
-        ps_r = ctx.enter_context(tc.psum_pool(name="ps_r", bufs=3))
+        ps_a = ctx.enter_context(tc.psum_pool(name="ps_a", bufs=A_BANKS))
+        ps_r = ctx.enter_context(tc.psum_pool(name="ps_r", bufs=2))
 
         x_sb = const.tile([P, UNITS, V], BF16)
         nc.sync.dma_start(out=x_sb[:], in_=x.rearrange("(u p) v -> p u v", p=P))
         wih_sb = ld.tile([P, G // P, V], BF16, tag="ld")
-        nc.sync.dma_start(out=wih_sb[:], in_=w_ih1.rearrange("(t p) v -> p t v", p=P))
+        for q in range(4):
+            nc.sync.dma_start(
+                out=wih_sb[:, 8 * q : 8 * q + 8, :],
+                in_=w_ih1[q * 1024 : (q + 1) * 1024, :].rearrange("(t p) v -> p t v", p=P),
+            )
         wi_b = const.tile([P, G], BF16)
-        nc.scalar.dma_start(out=wi_b[:], in_=lni_w1.partition_broadcast(P))
+        nc.sync.dma_start(out=wi_b[:], in_=lni_w1.partition_broadcast(P))
         bi_b = ld.tile([P, G], BF16, tag="ld")
-        nc.scalar.dma_start(out=bi_b[:], in_=lni_b1.partition_broadcast(P))
+        nc.sync.dma_start(out=bi_b[:], in_=lni_b1.partition_broadcast(P))
         bh_b = ld.tile([P, G], BF16, tag="ld")
-        nc.scalar.dma_start(out=bh_b[:], in_=lnh_b1.partition_broadcast(P))
+        nc.sync.dma_start(out=bh_b[:], in_=lnh_b1.partition_broadcast(P))
         h0_sb = ld.tile([P, UNITS, H], BF16, tag="ld")
         nc.sync.dma_start(out=h0_sb[:], in_=h0.rearrange("(u p) k -> p u k", p=P))
+        whh_words = {}
+        for m in range(4):
+            wland = big.tile([P, 8, H], BF16, tag="big")
+            for hh in range(2):
+                n = 2 * m + hh
+                nc.sync.dma_start(
+                    out=wland[:, 4 * hh : 4 * hh + 4, :],
+                    in_=w_hh1[n * BANK : (n + 1) * BANK, :].rearrange("(t p) k -> p t k", p=P),
+                )
+                whh_words[n] = wland[:].bitcast(F32)[:, 4 * hh : 4 * hh + 4, :]
 
         ident_b = const.tile([P, P], BF16)
         make_identity(nc, ident_b[:])
@@ -68,6 +83,7 @@ def tile_multilstm_pa_kernel(
         nc.scalar.copy(out=xT[:], in_=tpx[:].rearrange("p u b -> p (u b)"))
         nc.scalar.copy(out=xT_f[:], in_=tpx[:].rearrange("p u b -> p (u b)"))
         wihT = const.tile([P, G], BF16)
+        gram_ps = ps_r.tile([P, V], F32, tag="mmr")
         for q in range(4):
             tpw = ps_t.tile([P, 8, P], BF16, tag="tp")
             for j in range(8):
@@ -78,35 +94,25 @@ def tile_multilstm_pa_kernel(
                 func=ACT.Identity,
                 accum_out=gram[:, V + q : V + q + 1],
             )
-        gram_ps = ps_r.tile([P, V], F32, tag="mmr")
-        for t in range(G // P):
-            nc.tensor.matmul(
-                out=gram_ps[:], lhsT=wih_sb[:, t, :], rhs=wih_sb[:, t, :], start=(t == 0), stop=(t == G // P - 1)
-            )
+            for j in range(8):
+                t = 8 * q + j
+                nc.tensor.matmul(
+                    out=gram_ps[:], lhsT=wih_sb[:, t, :], rhs=wih_sb[:, t, :], start=(t == 0), stop=(t == G // P - 1)
+                )
         nc.scalar.copy(out=gram[:, 0:V], in_=gram_ps[:])
 
         bs = const.tile([P, G], F32)
-        for k in range(2):
-            cols = slice(k * 2048, (k + 1) * 2048)
-            nc.vector.tensor_tensor(out=bs[:, cols], in0=bi_b[:, cols], in1=bh_b[:, cols], op=ALU.add)
 
-        whh_tiles = {}
+        def bias_sum(k):
+            cols = slice(k * H, (k + 1) * H)
+            nc.gpsimd.tensor_tensor(out=bs[:, cols], in0=bi_b[:, cols], in1=bh_b[:, cols], op=ALU.add)
 
-        def load_whh(n):
-            whh_sb = ld.tile([P, 4, H], BF16, tag="ld")
-            nc.sync.dma_start(
-                out=whh_sb[:], in_=w_hh1[n * BANK : (n + 1) * BANK, :].rearrange("(t p) k -> p t k", p=P)
-            )
-            whh_tiles[n] = whh_sb
-
-        load_whh(0)
-        load_whh(1)
-        load_whh(2)
+        bias_sum(0)
 
         q4 = small.tile([P, UNITS], F32, tag="q4")
         mean4 = small.tile([P, UNITS], F32, tag="mean4")
         for u in range(UNITS):
-            y_ps = ps_r.tile([P, V + 4], F32, tag="mmr")
+            y_ps = ps_a.tile([P, V + 4], F32, tag="mma")
             nc.tensor.matmul(out=y_ps[:], lhsT=xT_f[:, u * P : (u + 1) * P], rhs=gram[:], start=True, stop=True)
             yjunk = small.tile([P, V], F32, tag="yjunk")
             nc.vector.scalar_tensor_tensor(
@@ -126,6 +132,14 @@ def tile_multilstm_pa_kernel(
         nc.gpsimd.tensor_scalar(out=veps4[:], in0=var4[:], scalar1=0.0, scalar2=EPS, op0=ALU.max, op1=ALU.add)
         rstd4 = small.tile([P, UNITS], F32, tag="rstd4")
         nc.gpsimd.tensor_tensor(out=rstd4[:], in0=veps4[:], in1=neghalf[:], op=ALU.pow)
+        for k in range(1, 4):
+            bias_sum(k)
+
+        wh_b = ld.tile([P, G], BF16, tag="ld")
+        nc.sync.dma_start(out=wh_b[:], in_=lnh_w1.partition_broadcast(P))
+        lwlb = ld.tile([P, 2, H], BF16, tag="ld")
+        nc.sync.dma_start(out=lwlb[:, 0, :], in_=lnc_w1.partition_broadcast(P))
+        nc.sync.dma_start(out=lwlb[:, 1, :], in_=lnc_b1.partition_broadcast(P))
 
         h_codes = const.tile([P, 2, B], U32, align_bytes=64)
         h_scales = const.tile([P, 2, B], U8, align_bytes=64)
@@ -157,9 +171,7 @@ def tile_multilstm_pa_kernel(
                 )
 
         def prep_whh(n):
-            transpose_rows(n, whh_tiles[n][:].bitcast(F32))
-            if n + 4 < NB:
-                load_whh(n + 4)
+            transpose_rows(n, whh_words[n])
 
         def quantise_whh(n):
             cols = slice(n * BANK, (n + 1) * BANK)
@@ -193,7 +205,7 @@ def tile_multilstm_pa_kernel(
         def t1_group(g):
             for k in range(4 * g, 4 * g + 4):
                 t1(k)
-                a_matmul(k + 3)
+                a_matmul(k + A_BANKS)
 
         def c1(g):
             u, half = divmod(g, 2)
@@ -334,48 +346,42 @@ def tile_multilstm_pa_kernel(
             side(u).tensor_tensor(out=gate(u, 3), in0=gate(u, 3), in1=gate(u, 0), op=ALU.mult)
             nc.sync.dma_start(out=out_0[u * P : (u + 1) * P, :], in_=gate(u, 3))
 
-        for k in range(3):
+        for k in range(A_BANKS):
             a_matmul(k)
-        transpose_rows("h", h0_sb[:].bitcast(F32))
-        load_whh(3)
-        prep_whh(0)
         t1_group(0)
-        c1(0)
-        quantise("h", h_codes, h_scales)
-        prep_whh(1)
-        quantise_whh(0)
-        prep_whh(2)
-        for g in range(1, 4):
-            t1_group(g)
-            quantise_whh(2 * g - 1)
-            prep_whh(2 * g + 1)
-            c1(g)
-            quantise_whh(2 * g)
-            if 2 * g + 2 < NB:
-                prep_whh(2 * g + 2)
-        wh_b = ld.tile([P, G], BF16, tag="ld")
-        nc.sync.dma_start(out=wh_b[:], in_=lnh_w1.partition_broadcast(P))
-        lwlb = ld.tile([P, 2, H], BF16, tag="ld")
-        nc.sync.dma_start(out=lwlb[:, 0, :], in_=lnc_w1.partition_broadcast(P))
-        nc.sync.dma_start(out=lwlb[:, 1, :], in_=lnc_b1.partition_broadcast(P))
+        transpose_rows("h", h0_sb[:].bitcast(F32))
         c0_sb = ld.tile([P, UNITS, H], BF16, tag="ld")
         nc.sync.dma_start(out=c0_sb[:], in_=c0.rearrange("(u p) k -> p u k", p=P))
-        t1_group(4)
+        prep_whh(0)
+        t1_group(1)
+        quantise("h", h_codes, h_scales)
+        prep_whh(1)
+        c1(0)
+        quantise_whh(0)
+        prep_whh(2)
+        c1(1)
+        for g in range(2, 5):
+            quantise_whh(2 * g - 3)
+            prep_whh(2 * g - 1)
+            t1_group(g)
+            quantise_whh(2 * g - 2)
+            if 2 * g < NB:
+                prep_whh(2 * g)
+            c1(g)
         quantise_whh(7)
         r_evict(0, range(NB))
         r_mean(0)
-        c1(4)
         t1_group(5)
+        c1(5)
+        t1_group(6)
         r_var(0, 0)
         r_var(0, 1)
-        c1(5)
         r_evict(1, range(NB))
         r_mean(1)
-        t1_group(6)
         c1(6)
+        t1_group(7)
         r_var(1, 0)
         r_var(1, 1)
-        t1_group(7)
         c1(7)
 
         for k in range(4):

@@ -36,9 +36,8 @@ def tile_multilstm_pa_kernel(
         grp_pool = ctx.enter_context(tc.tile_pool(name="grp", bufs=4))
         big = ctx.enter_context(tc.tile_pool(name="big", bufs=6))
         small = ctx.enter_context(tc.tile_pool(name="small", bufs=4))
-        ps_t = ctx.enter_context(tc.psum_pool(name="ps_t", bufs=2))
+        ps_x = ctx.enter_context(tc.psum_pool(name="ps_x", bufs=4))
         ps_a = ctx.enter_context(tc.psum_pool(name="ps_a", bufs=A_BANKS))
-        ps_r = ctx.enter_context(tc.psum_pool(name="ps_r", bufs=2))
 
         x_sb = const.tile([P, UNITS, V], BF16)
         nc.sync.dma_start(out=x_sb[:], in_=x.rearrange("(u p) v -> p u v", p=P))
@@ -77,15 +76,15 @@ def tile_multilstm_pa_kernel(
         xT = const.tile([P, B], BF16)
         xT_f = const.tile([P, B], F32)
         gram = const.tile([P, V + 4], F32)
-        tpx = ps_t.tile([P, UNITS, P], BF16, tag="tp")
+        tpx = ps_x.tile([P, UNITS, P], BF16, tag="x")
         for u in range(UNITS):
             nc.tensor.transpose(tpx[:, u, :], x_sb[:, u, :], ident_b[:])
         nc.scalar.copy(out=xT[:], in_=tpx[:].rearrange("p u b -> p (u b)"))
         nc.scalar.copy(out=xT_f[:], in_=tpx[:].rearrange("p u b -> p (u b)"))
         wihT = const.tile([P, G], BF16)
-        gram_ps = ps_r.tile([P, V], F32, tag="mmr")
+        gram_ps = ps_a.tile([P, V], F32, tag="mma")
         for q in range(4):
-            tpw = ps_t.tile([P, 8, P], BF16, tag="tp")
+            tpw = ps_x.tile([P, 8, P], BF16, tag="x")
             for j in range(8):
                 nc.tensor.transpose(tpw[:, j, :], wih_sb[:, 8 * q + j, :], ident_b[:])
             nc.scalar.activation(
@@ -152,7 +151,7 @@ def tile_multilstm_pa_kernel(
                 grp = grp_pool.tile([P, 4 * BANK], BF16, tag="grp", align_bytes=64)
                 grpw = grp[:].bitcast(F32).rearrange("p (r s) -> p r s", s=2)
                 for half in range(2):
-                    tp = ps_t.tile([P, 2, 256], F32, tag="tp")
+                    tp = ps_x.tile([P, 2, 256], F32, tag="x")
                     for s in range(2):
                         for j in range(2):
                             lo = 256 * c + 128 * s
@@ -227,7 +226,7 @@ def tile_multilstm_pa_kernel(
                 st[("s1", u)] = s1
             for n in banks:
                 cols = slice(n * BANK, (n + 1) * BANK)
-                acc = ps_r.tile([P, BANK], F32, tag="mmr")
+                acc = ps_x.tile([P, BANK], F32, tag="x")
                 for c in range(2):
                     nc.tensor.matmul_mx(
                         out=acc[:],
@@ -399,6 +398,7 @@ def tile_multilstm_pa_kernel(
                 r_evict(u + 2, range(0, 6))
             if nxt:
                 t2(u + 1, 0)
+                t2(u + 1, 1)
             m1(u)
             m2_cp(u)
             c_var(u)
@@ -406,7 +406,6 @@ def tile_multilstm_pa_kernel(
                 r_evict(u + 2, range(6, NB))
                 r_mean(u + 2)
             if nxt:
-                t2(u + 1, 1)
                 t2(u + 1, 2)
             cy1(u)
             if nxt:

@@ -247,27 +247,23 @@ def tile_multilstm_pa_kernel(
             nc.scalar.activation(
                 out=s1junk[:], in_=st[("s1", u)][:], func=ACT.Identity, scale=-1.0 / G, accum_out=negmean[:]
             )
-            s1junk2 = small.tile([P, NB], F32, tag="s1junk2")
-            negmean64 = small.tile([P, 1], F32, tag="negmean64")
-            nc.scalar.activation(
-                out=s1junk2[:], in_=st[("s1", u)][:], func=ACT.Identity, scale=-1.0 / (G * 64.0), accum_out=negmean64[:]
-            )
             ssq = small.tile([P, 2], F32, tag="ssq")
             st[("negmean", u)] = negmean
-            st[("negmean64", u)] = negmean64
             st[("ssq", u)] = ssq
 
         def r_var(u, k):
             junk = grp_pool.tile([P, 2048], BF16, tag="grp", align_bytes=64)
             nc.scalar.activation(
                 out=junk[:], in_=r_tiles[u][:, k * 2048 : (k + 1) * 2048], func=ACT.Square,
-                bias=st[("negmean64", u)][:, 0:1], scale=1.0 / 64.0, accum_out=st[("ssq", u)][:, k : k + 1],
+                bias=st[("negmean", u)][:, 0:1], scale=1.0, accum_out=st[("ssq", u)][:, k : k + 1],
             )
             if k == 1:
                 ssq = st[("ssq", u)]
                 vjunk = small.tile([P, 2], F32, tag="vjunk")
                 veps = small.tile([P, 1], F32, tag="veps")
-                nc.scalar.activation(out=vjunk[:], in_=ssq[:], func=ACT.Identity, bias=EPS / 2.0, accum_out=veps[:])
+                nc.scalar.activation(
+                    out=vjunk[:], in_=ssq[:], func=ACT.Identity, bias=EPS / 2.0, scale=1.0 / G, accum_out=veps[:]
+                )
                 rstd = small.tile([P, 1], F32, tag="rstd")
                 nc.gpsimd.tensor_tensor(out=rstd[:], in0=veps[:], in1=neghalf[:, 0:1], op=ALU.pow)
                 st[("rstd", u)] = rstd
@@ -305,22 +301,19 @@ def tile_multilstm_pa_kernel(
                 out=gate(u, 0), in0=gate(u, 0), scalar=1.0, in1=gate(u, 1), op0=ALU.mult, op1=ALU.add,
                 accum_out=csum[:],
             )
-            cneg = small.tile([P, 2], F32, tag="cneg")
-            nc.vector.tensor_scalar(out=cneg[:, 0:1], in0=csum[:], scalar1=-1.0 / H, scalar2=None, op0=ALU.mult)
-            nc.vector.tensor_scalar(
-                out=cneg[:, 1:2], in0=csum[:], scalar1=-1.0 / (H * 32.0), scalar2=None, op0=ALU.mult
-            )
+            cneg = small.tile([P, 1], F32, tag="cneg")
+            nc.vector.tensor_scalar(out=cneg[:], in0=csum[:], scalar1=-1.0 / H, scalar2=None, op0=ALU.mult)
             st[("cneg", u)] = cneg
 
         def c_var(u):
             cssq = small.tile([P, 1], F32, tag="cssq")
             cjunk = grp_pool.tile([P, 2048], BF16, tag="grp", align_bytes=64)
             nc.scalar.activation(
-                out=cjunk[:, 0:H], in_=gate(u, 0), func=ACT.Square, bias=st[("cneg", u)][:, 1:2], scale=1.0 / 32.0,
+                out=cjunk[:, 0:H], in_=gate(u, 0), func=ACT.Square, bias=st[("cneg", u)][:, 0:1], scale=1.0,
                 accum_out=cssq[:],
             )
             cveps = small.tile([P, 1], F32, tag="cveps")
-            nc.scalar.activation(out=cveps[:], in_=cssq[:], func=ACT.Identity, bias=EPS)
+            nc.scalar.activation(out=cveps[:], in_=cssq[:], func=ACT.Identity, bias=EPS, scale=1.0 / H)
             crstd = small.tile([P, 1], F32, tag="crstd")
             nc.gpsimd.tensor_tensor(out=crstd[:], in0=cveps[:], in1=neghalf[:, 0:1], op=ALU.pow)
             st[("crstd", u)] = crstd
@@ -337,6 +330,23 @@ def tile_multilstm_pa_kernel(
                 op0=ALU.mult, op1=ALU.add,
             )
             nc.sync.dma_start(out=out_1[u * P : (u + 1) * P, :], in_=gate(u, 1))
+
+        def half(u, k, hh):
+            return r_tiles[u][:, k * H + hh * BANK : k * H + (hh + 1) * BANK]
+
+        def cy_half(u, hh):
+            cols = slice(hh * BANK, (hh + 1) * BANK)
+            nc.vector.scalar_tensor_tensor(
+                out=half(u, 1, hh), in0=half(u, 2, hh), scalar=st[("crstd", u)][:, 0:1], in1=lwlb[:, 1, cols],
+                op0=ALU.mult, op1=ALU.add,
+            )
+            nc.sync.dma_start(out=out_1[u * P : (u + 1) * P, cols], in_=half(u, 1, hh))
+            nc.scalar.activation(out=half(u, 0, hh), in_=half(u, 1, hh), func=ACT.Tanh)
+
+        def hy_half(u, hh):
+            cols = slice(hh * BANK, (hh + 1) * BANK)
+            nc.vector.tensor_tensor(out=half(u, 3, hh), in0=half(u, 3, hh), in1=half(u, 0, hh), op=ALU.mult)
+            nc.sync.dma_start(out=out_0[u * P : (u + 1) * P, cols], in_=half(u, 3, hh))
 
         def c_tanh(u):
             nc.scalar.activation(out=gate(u, 0), in_=gate(u, 1), func=ACT.Tanh)
@@ -385,8 +395,7 @@ def tile_multilstm_pa_kernel(
 
         for k in range(4):
             t2(0, k)
-        for u in range(UNITS):
-            nxt = u + 1 < UNITS
+        for u in range(UNITS - 1):
             far = u + 2 < UNITS
             c2(u, 1)
             c2(u, 0)
@@ -396,24 +405,34 @@ def tile_multilstm_pa_kernel(
                 hy(u - 1)
             if far:
                 r_evict(u + 2, range(0, 6))
-            if nxt:
-                t2(u + 1, 0)
-                t2(u + 1, 1)
+            t2(u + 1, 0)
+            t2(u + 1, 1)
             m1(u)
             m2_cp(u)
             c_var(u)
             if far:
                 r_evict(u + 2, range(6, NB))
                 r_mean(u + 2)
-            if nxt:
-                t2(u + 1, 2)
+            t2(u + 1, 2)
             cy1(u)
-            if nxt:
-                t2(u + 1, 3)
+            t2(u + 1, 3)
             if far:
                 r_var(u + 2, 0)
             cy(u)
             c_tanh(u)
             if far:
                 r_var(u + 2, 1)
-        hy(UNITS - 1)
+        last = UNITS - 1
+        c2(last, 1)
+        c2(last, 0)
+        c2(last, 2)
+        c2(last, 3)
+        m1(last)
+        m2_cp(last)
+        c_var(last)
+        cy1(last)
+        hy(last - 1)
+        cy_half(last, 0)
+        cy_half(last, 1)
+        hy_half(last, 0)
+        hy_half(last, 1)

from contextlib import ExitStack

import concourse.mybir as mybir
from concourse.masks import make_identity

F32 = mybir.dt.float32
BF16 = mybir.dt.bfloat16
U32 = mybir.dt.uint32
U8 = mybir.dt.uint8
FP8X4 = mybir.dt.float8_e4m3fn_x4
ACT = mybir.ActivationFunctionType
ALU = mybir.AluOpType

P = 128
B, V, H = 512, 128, 1024
G = 4 * H
EPS = 1e-5
UNITS = B // P
BANK = 512
NB = G // BANK
FLOPS = 2 * B * G * (H + V)
PIN = True
A_BANKS = 4
POOL_UNITS = ()


def tile_multilstm_pa_kernel(
    tc, x, h0, c0, w_ih1, w_hh1, lni_w1, lni_b1, lnh_w1, lnh_b1, lnc_w1, lnc_b1, out_0, out_1
):
    nc = tc.nc
    with ExitStack() as ctx:
        if PIN:
            ctx.enter_context(tc.manual_schedule())
        const = ctx.enter_context(tc.tile_pool(name="const", bufs=1))
        ld = ctx.enter_context(tc.tile_pool(name="ld", bufs=4))
        grp_pool = ctx.enter_context(tc.tile_pool(name="grp", bufs=4))
        big = ctx.enter_context(tc.tile_pool(name="big", bufs=6))
        small = ctx.enter_context(tc.tile_pool(name="small", bufs=4))
        ps_x = ctx.enter_context(tc.psum_pool(name="ps_x", bufs=4))
        ps_a = ctx.enter_context(tc.psum_pool(name="ps_a", bufs=A_BANKS))

        x_sb = const.tile([P, UNITS, V], BF16)
        nc.sync.dma_start(out=x_sb[:], in_=x.rearrange("(u p) v -> p u v", p=P))
        wih_sb = ld.tile([P, G // P, V], BF16, tag="ld")
        for q in range(4):
            nc.sync.dma_start(
                out=wih_sb[:, 8 * q : 8 * q + 8, :],
                in_=w_ih1[q * 1024 : (q + 1) * 1024, :].rearrange("(t p) v -> p t v", p=P),
            )
        wi_b = const.tile([P, G], BF16)
        nc.sync.dma_start(out=wi_b[:], in_=lni_w1.partition_broadcast(P))
        bi_b = ld.tile([P, G], BF16, tag="ld")
        nc.sync.dma_start(out=bi_b[:], in_=lni_b1.partition_broadcast(P))
        bh_b = ld.tile([P, G], BF16, tag="ld")
        nc.sync.dma_start(out=bh_b[:], in_=lnh_b1.partition_broadcast(P))
        h0_sb = ld.tile([P, UNITS, H], BF16, tag="ld")
        nc.sync.dma_start(out=h0_sb[:], in_=h0.rearrange("(u p) k -> p u k", p=P))
        whh_words = {}
        for m in range(4):
            wland = big.tile([P, 8, H], BF16, tag="big")
            for hh in range(2):
                n = 2 * m + hh
                nc.sync.dma_start(
                    out=wland[:, 4 * hh : 4 * hh + 4, :],
                    in_=w_hh1[n * BANK : (n + 1) * BANK, :].rearrange("(t p) k -> p t k", p=P),
                )
                whh_words[n] = wland[:].bitcast(F32)[:, 4 * hh : 4 * hh + 4, :]

        ident_b = const.tile([P, P], BF16)
        make_identity(nc, ident_b[:])
        ident_f = const.tile([P, P], F32)
        make_identity(nc, ident_f[:])
        neghalf = const.tile([P, UNITS], F32)
        nc.vector.memset(neghalf[:], -0.5)

        xT = const.tile([P, B], BF16)
        xT_f = const.tile([P, B], F32)
        gram = const.tile([P, V + 4], F32)
        tpx = ps_x.tile([P, UNITS, P], BF16, tag="x")
        for u in range(UNITS):
            nc.tensor.transpose(tpx[:, u, :], x_sb[:, u, :], ident_b[:])
        nc.scalar.copy(out=xT[:], in_=tpx[:].rearrange("p u b -> p (u b)"))
        nc.scalar.copy(out=xT_f[:], in_=tpx[:].rearrange("p u b -> p (u b)"))
        wihT = const.tile([P, G], BF16)
        gram_ps = ps_a.tile([P, V], F32, tag="mma")
        for q in range(4):
            tpw = ps_x.tile([P, 8, P], BF16, tag="x")
            for j in range(8):
                nc.tensor.transpose(tpw[:, j, :], wih_sb[:, 8 * q + j, :], ident_b[:])
            nc.scalar.activation(
                out=wihT[:, q * 1024 : (q + 1) * 1024],
                in_=tpw[:].rearrange("p j g -> p (j g)"),
                func=ACT.Identity,
                accum_out=gram[:, V + q : V + q + 1],
            )
            for j in range(8):
                t = 8 * q + j
                nc.tensor.matmul(
                    out=gram_ps[:], lhsT=wih_sb[:, t, :], rhs=wih_sb[:, t, :], start=(t == 0), stop=(t == G // P - 1)
                )
        nc.scalar.copy(out=gram[:, 0:V], in_=gram_ps[:])

        bs = const.tile([P, G], F32)

        def bias_sum(k):
            cols = slice(k * H, (k + 1) * H)
            nc.gpsimd.tensor_tensor(out=bs[:, cols], in0=bi_b[:, cols], in1=bh_b[:, cols], op=ALU.add)

        bias_sum(0)

        q4 = small.tile([P, UNITS], F32, tag="q4")
        mean4 = small.tile([P, UNITS], F32, tag="mean4")
        for u in range(UNITS):
            y_ps = ps_a.tile([P, V + 4], F32, tag="mma")
            nc.tensor.matmul(out=y_ps[:], lhsT=xT_f[:, u * P : (u + 1) * P], rhs=gram[:], start=True, stop=True)
            yjunk = small.tile([P, V], F32, tag="yjunk")
            nc.vector.scalar_tensor_tensor(
                out=yjunk[:], in0=y_ps[:, 0:V], scalar=1.0 / G, in1=x_sb[:, u, :], op0=ALU.mult, op1=ALU.mult,
                accum_out=q4[:, u : u + 1],
            )
            mjunk = small.tile([P, 4], F32, tag="mjunk")
            nc.vector.tensor_scalar(
                out=mjunk[:], in0=y_ps[:, V : V + 4], scalar1=1.0 / G, scalar2=None, op0=ALU.mult, op1=ALU.add,
                accum_out=mean4[:, u : u + 1],
            )
        msq4 = small.tile([P, UNITS], F32, tag="msq4")
        nc.vector.tensor_tensor(out=msq4[:], in0=mean4[:], in1=mean4[:], op=ALU.mult)
        var4 = small.tile([P, UNITS], F32, tag="var4")
        nc.vector.tensor_tensor(out=var4[:], in0=q4[:], in1=msq4[:], op=ALU.subtract)
        veps4 = small.tile([P, UNITS], F32, tag="veps4")
        nc.gpsimd.tensor_scalar(out=veps4[:], in0=var4[:], scalar1=0.0, scalar2=EPS, op0=ALU.max, op1=ALU.add)
        rstd4 = small.tile([P, UNITS], F32, tag="rstd4")
        nc.gpsimd.tensor_tensor(out=rstd4[:], in0=veps4[:], in1=neghalf[:], op=ALU.pow)
        for k in range(1, 4):
            bias_sum(k)

        wh_b = ld.tile([P, G], BF16, tag="ld")
        nc.sync.dma_start(out=wh_b[:], in_=lnh_w1.partition_broadcast(P))
        lwlb = ld.tile([P, 2, H], BF16, tag="ld")
        nc.sync.dma_start(out=lwlb[:, 0, :], in_=lnc_w1.partition_broadcast(P))
        nc.sync.dma_start(out=lwlb[:, 1, :], in_=lnc_b1.partition_broadcast(P))

        h_codes = const.tile([P, 2, B], U32, align_bytes=64)
        h_scales = const.tile([P, 2, B], U8, align_bytes=64)
        w_codes = const.tile([P, 2, G], U32, align_bytes=64)
        w_scales = const.tile([P, 2, G], U8, align_bytes=64)
        grp_tiles = {}

        def transpose_rows(key, src_words):
            for c in range(2):
                grp = grp_pool.tile([P, 4 * BANK], BF16, tag="grp", align_bytes=64)
                grpw = grp[:].bitcast(F32).rearrange("p (r s) -> p r s", s=2)
                for half in range(2):
                    tp = ps_x.tile([P, 2, 256], F32, tag="x")
                    for s in range(2):
                        for j in range(2):
                            lo = 256 * c + 128 * s
                            nc.tensor.transpose(
                                tp[:, s, j * P : (j + 1) * P], src_words[:, 2 * half + j, lo : lo + P], ident_f[:]
                            )
                    nc.scalar.copy(
                        out=grpw[:, half * 256 : (half + 1) * 256, :], in_=tp[:].rearrange("p s r -> p r s")
                    )
                grp_tiles[(key, c)] = grp

        def quantise(key, codes, scales):
            for c in range(2):
                nc.vector.quantize_mx(
                    out=codes[:, c, :].bitcast(FP8X4), scales=scales[:, c, :], in_=grp_tiles[(key, c)][:]
                )

        def prep_whh(n):
            transpose_rows(n, whh_words[n])

        def quantise_whh(n):
            cols = slice(n * BANK, (n + 1) * BANK)
            quantise(n, w_codes[:, :, cols], w_scales[:, :, cols])

        a_tiles = {}
        a_banks = {}

        def a_matmul(k):
            if k >= UNITS * NB:
                return
            u, n = divmod(k, NB)
            acc = ps_a.tile([P, BANK], F32, tag="mma")
            nc.tensor.matmul(
                out=acc[:], lhsT=xT[:, u * P : (u + 1) * P], rhs=wihT[:, n * BANK : (n + 1) * BANK],
                start=True, stop=True,
            )
            a_banks[k] = acc

        def t1(k):
            u, n = divmod(k, NB)
            if n == 0:
                a_new = big.tile([P, G], F32, tag="big")
                a_tiles[u] = a_new
            cols = slice(n * BANK, (n + 1) * BANK)
            nc.vector.scalar_tensor_tensor(
                out=a_tiles[u][:, cols], in0=a_banks[k][:], scalar=mean4[:, u : u + 1], in1=wi_b[:, cols],
                op0=ALU.subtract, op1=ALU.mult,
            )

        def t1_group(g):
            for k in range(4 * g, 4 * g + 4):
                t1(k)
                a_matmul(k + A_BANKS)

        def c1(g):
            u, half = divmod(g, 2)
            cols = slice(half * 2048, (half + 1) * 2048)
            nc.vector.scalar_tensor_tensor(
                out=a_tiles[u][:, cols], in0=a_tiles[u][:, cols], scalar=rstd4[:, u : u + 1], in1=bs[:, cols],
                op0=ALU.mult, op1=ALU.add,
            )

        r_tiles = {}
        st = {}

        def r_evict(u, banks):
            rows = slice(u * P, (u + 1) * P)
            if u not in r_tiles:
                r_new = big.tile([P, G], F32, tag="big")
                r_tiles[u] = r_new
                s1 = small.tile([P, NB], F32, tag="s1")
                st[("s1", u)] = s1
            for n in banks:
                cols = slice(n * BANK, (n + 1) * BANK)
                acc = ps_x.tile([P, BANK], F32, tag="x")
                for c in range(2):
                    nc.tensor.matmul_mx(
                        out=acc[:],
                        lhsT=h_codes[:, c, rows].bitcast(FP8X4),
                        lhsT_scale=h_scales[:, c, rows],
                        rhs=w_codes[:, c, cols].bitcast(FP8X4),
                        rhs_scale=w_scales[:, c, cols],
                        start=(c == 0),
                        stop=(c == 1),
                    )
                nc.scalar.activation(
                    out=r_tiles[u][:, cols], in_=acc[:], func=ACT.Identity, accum_out=st[("s1", u)][:, n : n + 1]
                )

        def r_mean(u):
            s1junk = small.tile([P, NB], F32, tag="s1junk")
            negmean = small.tile([P, 1], F32, tag="negmean")
            nc.scalar.activation(
                out=s1junk[:], in_=st[("s1", u)][:], func=ACT.Identity, scale=-1.0 / G, accum_out=negmean[:]
            )
            ssq = small.tile([P, 2], F32, tag="ssq")
            st[("negmean", u)] = negmean
            st[("ssq", u)] = ssq

        def r_var(u, k):
            junk = grp_pool.tile([P, 2048], BF16, tag="grp", align_bytes=64)
            nc.scalar.activation(
                out=junk[:], in_=r_tiles[u][:, k * 2048 : (k + 1) * 2048], func=ACT.Square,
                bias=st[("negmean", u)][:, 0:1], scale=1.0, accum_out=st[("ssq", u)][:, k : k + 1],
            )
            if k == 1:
                ssq = st[("ssq", u)]
                vjunk = small.tile([P, 2], F32, tag="vjunk")
                veps = small.tile([P, 1], F32, tag="veps")
                nc.scalar.activation(
                    out=vjunk[:], in_=ssq[:], func=ACT.Identity, bias=EPS / 2.0, scale=1.0 / G, accum_out=veps[:]
                )
                rstd = small.tile([P, 1], F32, tag="rstd")
                nc.gpsimd.tensor_tensor(out=rstd[:], in0=veps[:], in1=neghalf[:, 0:1], op=ALU.pow)
                st[("rstd", u)] = rstd

        def t2(u, k):
            cols = slice(k * H, (k + 1) * H)
            nc.vector.scalar_tensor_tensor(
                out=r_tiles[u][:, cols], in0=r_tiles[u][:, cols], scalar=st[("negmean", u)][:, 0:1],
                in1=wh_b[:, cols], op0=ALU.add, op1=ALU.mult,
            )

        funcs = [ACT.Sigmoid, ACT.Sigmoid, ACT.Tanh, ACT.Sigmoid]

        def c2(u, k):
            cols = slice(k * H, (k + 1) * H)
            nc.vector.scalar_tensor_tensor(
                out=r_tiles[u][:, cols], in0=r_tiles[u][:, cols], scalar=st[("rstd", u)][:, 0:1],
                in1=a_tiles[u][:, cols], op0=ALU.mult, op1=ALU.add,
            )
            nc.scalar.activation(out=r_tiles[u][:, cols], in_=r_tiles[u][:, cols], func=funcs[k])

        def gate(u, k):
            return r_tiles[u][:, k * H : (k + 1) * H]

        def side(u):
            return nc.gpsimd if u in POOL_UNITS else nc.vector

        def m1(u):
            side(u).tensor_tensor(out=gate(u, 1), in0=gate(u, 1), in1=c0_sb[:, u, :], op=ALU.mult)

        def m2_cp(u):
            nc.vector.tensor_tensor(out=gate(u, 0), in0=gate(u, 0), in1=gate(u, 2), op=ALU.mult)
            csum = small.tile([P, 1], F32, tag="csum")
            nc.vector.scalar_tensor_tensor(
                out=gate(u, 0), in0=gate(u, 0), scalar=1.0, in1=gate(u, 1), op0=ALU.mult, op1=ALU.add,
                accum_out=csum[:],
            )
            cneg = small.tile([P, 1], F32, tag="cneg")
            nc.vector.tensor_scalar(out=cneg[:], in0=csum[:], scalar1=-1.0 / H, scalar2=None, op0=ALU.mult)
            st[("cneg", u)] = cneg

        def c_var(u):
            cssq = small.tile([P, 1], F32, tag="cssq")
            cjunk = grp_pool.tile([P, 2048], BF16, tag="grp", align_bytes=64)
            nc.scalar.activation(
                out=cjunk[:, 0:H], in_=gate(u, 0), func=ACT.Square, bias=st[("cneg", u)][:, 0:1], scale=1.0,
                accum_out=cssq[:],
            )
            cveps = small.tile([P, 1], F32, tag="cveps")
            nc.scalar.activation(out=cveps[:], in_=cssq[:], func=ACT.Identity, bias=EPS, scale=1.0 / H)
            crstd = small.tile([P, 1], F32, tag="crstd")
            nc.gpsimd.tensor_tensor(out=crstd[:], in0=cveps[:], in1=neghalf[:, 0:1], op=ALU.pow)
            st[("crstd", u)] = crstd

        def cy1(u):
            nc.vector.scalar_tensor_tensor(
                out=gate(u, 2), in0=gate(u, 0), scalar=st[("cneg", u)][:, 0:1], in1=lwlb[:, 0, :],
                op0=ALU.add, op1=ALU.mult,
            )

        def cy(u):
            nc.vector.scalar_tensor_tensor(
                out=gate(u, 1), in0=gate(u, 2), scalar=st[("crstd", u)][:, 0:1], in1=lwlb[:, 1, :],
                op0=ALU.mult, op1=ALU.add,
            )
            nc.sync.dma_start(out=out_1[u * P : (u + 1) * P, :], in_=gate(u, 1))

        def half(u, k, hh):
            return r_tiles[u][:, k * H + hh * BANK : k * H + (hh + 1) * BANK]

        def cy_half(u, hh):
            cols = slice(hh * BANK, (hh + 1) * BANK)
            nc.vector.scalar_tensor_tensor(
                out=half(u, 1, hh), in0=half(u, 2, hh), scalar=st[("crstd", u)][:, 0:1], in1=lwlb[:, 1, cols],
                op0=ALU.mult, op1=ALU.add,
            )
            nc.sync.dma_start(out=out_1[u * P : (u + 1) * P, cols], in_=half(u, 1, hh))
            nc.scalar.activation(out=half(u, 0, hh), in_=half(u, 1, hh), func=ACT.Tanh)

        def hy_half(u, hh):
            cols = slice(hh * BANK, (hh + 1) * BANK)
            nc.vector.tensor_tensor(out=half(u, 3, hh), in0=half(u, 3, hh), in1=half(u, 0, hh), op=ALU.mult)
            nc.sync.dma_start(out=out_0[u * P : (u + 1) * P, cols], in_=half(u, 3, hh))

        def c_tanh(u):
            nc.scalar.activation(out=gate(u, 0), in_=gate(u, 1), func=ACT.Tanh)

        def hy(u):
            side(u).tensor_tensor(out=gate(u, 3), in0=gate(u, 3), in1=gate(u, 0), op=ALU.mult)
            nc.sync.dma_start(out=out_0[u * P : (u + 1) * P, :], in_=gate(u, 3))

        for k in range(A_BANKS):
            a_matmul(k)
        t1_group(0)
        transpose_rows("h", h0_sb[:].bitcast(F32))
        c0_sb = ld.tile([P, UNITS, H], BF16, tag="ld")
        nc.sync.dma_start(out=c0_sb[:], in_=c0.rearrange("(u p) k -> p u k", p=P))
        prep_whh(0)
        t1_group(1)
        quantise("h", h_codes, h_scales)
        prep_whh(1)
        c1(0)
        quantise_whh(0)
        prep_whh(2)
        c1(1)
        for g in range(2, 5):
            quantise_whh(2 * g - 3)
            prep_whh(2 * g - 1)
            t1_group(g)
            quantise_whh(2 * g - 2)
            if 2 * g < NB:
                prep_whh(2 * g)
            c1(g)
        quantise_whh(7)
        r_evict(0, range(NB))
        r_mean(0)
        t1_group(5)
        c1(5)
        t1_group(6)
        r_var(0, 0)
        r_var(0, 1)
        r_evict(1, range(NB))
        r_mean(1)
        c1(6)
        t1_group(7)
        r_var(1, 0)
        r_var(1, 1)
        c1(7)

        for k in range(4):
            t2(0, k)
        for u in range(UNITS - 1):
            far = u + 2 < UNITS
            c2(u, 1)
            c2(u, 0)
            c2(u, 2)
            c2(u, 3)
            if u > 0:
                hy(u - 1)
            if far:
                r_evict(u + 2, range(0, 6))
            t2(u + 1, 0)
            t2(u + 1, 1)
            m1(u)
            m2_cp(u)
            c_var(u)
            if far:
                r_evict(u + 2, range(6, NB))
                r_mean(u + 2)
            t2(u + 1, 2)
            cy1(u)
            t2(u + 1, 3)
            if far:
                r_var(u + 2, 0)
            cy(u)
            c_tanh(u)
            if far:
                r_var(u + 2, 1)
        last = UNITS - 1
        c2(last, 1)
        c2(last, 0)
        c2(last, 2)
        c2(last, 3)
        m1(last)
        m2_cp(last)
        c_var(last)
        cy1(last)
        hy(last - 1)
        cy_half(last, 0)
        cy_half(last, 1)
        hy_half(last, 0)
        hy_half(last, 1)
